import numpy as np
import ml_dtypes


def mxq(x, axis, fmt="e4m3"):
    dtype, down = {"e4m3": (ml_dtypes.float8_e4m3fn, 7), "e5m2": (ml_dtypes.float8_e5m2, 14)}[fmt]
    v = np.moveaxis(np.asarray(x, np.float32).astype(ml_dtypes.bfloat16).astype(np.float64), axis, -1)
    blocks = v.reshape(v.shape[:-1] + (-1, 32))
    amax = np.abs(blocks).max(-1, keepdims=True)
    byte = np.maximum(np.where(amax > 0, np.frexp(amax)[1] - 1 + 127, 0) - down, 1)
    scale = np.exp2(byte - 127.0)
    codes = (blocks / scale).astype(np.float32).astype(dtype).astype(np.float64)
    return np.moveaxis((codes * scale).reshape(v.shape), -1, axis)


WIDE = False


def mx_kscale(k):
    if not WIDE:
        return np.ones(k)
    levels = np.array([10, -10, 5, -5, 0])
    if k % 512:
        return np.exp2(np.random.permutation(np.resize(levels, k // 32))).repeat(32)
    a = np.empty((k // 512, 16))
    for p in range(k // 512):
        a[p, :8] = np.random.permutation(np.resize(levels, 8))
        for g in range(8):
            far = levels[np.abs(levels - a[p, g]) >= 10]
            a[p, g + 8] = far[np.random.randint(len(far))]
    return np.exp2(a.ravel()).repeat(32)


BF16 = ml_dtypes.bfloat16


def bf(x):
    return np.asarray(x, np.float32).astype(BF16)


def f64(x):
    return np.asarray(x).astype(np.float64)


E2M1 = np.array([0.0, 0.5, 1.0, 1.5, 2.0, 3.0, 4.0, 6.0, -0.0, -0.5, -1.0, -1.5, -2.0, -3.0, -4.0, -6.0])


def pack_weight(w, fmt):
    k, n = w.shape
    w = f64(bf(w)).reshape(k // 32, 32, n)
    amax = np.abs(w).max(1)
    if fmt == "e4m3":
        byte = np.frexp(amax)[1] - 1 + 127 - 7
    else:
        mant, ex = np.frexp(amax / 6.0)
        byte = np.where(mant > 0.5, ex, ex - 1) + 127
    byte = np.clip(np.where(amax > 0, byte, 1), 1, 254)
    scaled = (w * np.exp2(127.0 - byte)[:, None, :]).reshape(k, n).astype(np.float32)
    by_word = np.ascontiguousarray(scaled.reshape(k // 512, 128, 4, n).transpose(0, 1, 3, 2))
    if fmt == "e4m3":
        words = by_word.astype(ml_dtypes.float8_e4m3fn).view(np.uint8)
    else:
        c = by_word.astype(ml_dtypes.float4_e2m1fn).view(np.uint8) & 0xF
        words = c[..., 0::2] | (c[..., 1::2] << 4)
    return np.ascontiguousarray(words), np.ascontiguousarray(byte.astype(np.uint8).reshape(k // 512, 16, n))


def unpack_weight(words, scales, fmt):
    g, p, n, _ = words.shape
    if fmt == "e4m3":
        vals = np.ascontiguousarray(words).view(ml_dtypes.float8_e4m3fn).astype(np.float64)
    else:
        nib = np.empty((g, p, n, 4), np.uint8)
        nib[..., 0::2] = words & 0xF
        nib[..., 1::2] = words >> 4
        vals = E2M1[nib]
    vals = vals * np.repeat(np.exp2(scales.astype(np.float64) - 127.0), 8, axis=1)[..., None]
    return vals.transpose(0, 1, 3, 2).reshape(g * 512, n)
def pack4(w):
    words, scales = pack_weight(w, "e2m1")
    return words.reshape(words.shape[0], 128, -1), scales


def unpack4(words, scales):
    return unpack_weight(words.reshape(words.shape[0], 128, -1, 2), scales, "e2m1")


B, S, D, H, DN, DR, DV, QL, KVL, LBLK = 4, 2048, 512, 4, 32, 32, 128, 512, 512, 64
DQ = DN + DR


def silu(v):
    return v / (1.0 + np.exp(-v))


def apply_rope(x, fc):
    xr, xi = x[..., 0::2], x[..., 1::2]
    cos = fc[None, :, None, :, 0]
    sin = fc[None, :, None, :, 1]
    yr = xr * cos - xi * sin
    yi = xr * sin + xi * cos
    return np.stack([yr, yi], axis=-1).reshape(x.shape)


def eta(t):
    m = t.reshape(t.shape[0], H, -1).max(-1)
    m = np.where(m == 0, 1e-6, m)
    return np.minimum(10.0 / m, 1.0)


def draw0():
    s, t = mx_kscale(D), mx_kscale(QL)
    amp = np.linspace(0.5, 1.5, S)[None, :, None]
    ang = np.arange(S)[:, None] / 10000.0 ** (np.arange(0, DR, 2) / DR)[None, :]
    x = bf(np.random.standard_normal((B, S, D)) * amp * s)
    wq_a = np.random.standard_normal((QL, D)) / np.sqrt(D) / s[None, :] * t[:, None]
    wq_b = np.random.standard_normal((H * DQ, QL)) * 2.5 / np.sqrt(QL) / t[None, :]
    wq_a_words, wq_a_scales = pack4(wq_a.T)
    wq_b_words, wq_b_scales = pack4(wq_b.T)
    return {"x": x,
            "freqs_cis": bf(np.stack([np.cos(ang), np.sin(ang)], axis=-1)),
            "wq_a_words": wq_a_words, "wq_a_scales": wq_a_scales,
            "wq_b_words": wq_b_words, "wq_b_scales": wq_b_scales}


def core(x, freqs_cis, wq_a_words, wq_a_scales, wq_b_words, wq_b_scales):
    q_c = mxq(f64(x), 2, "e4m3") @ unpack4(wq_a_words, wq_a_scales)
    q = (mxq(q_c, 2, "e4m3") @ unpack4(wq_b_words, wq_b_scales)).reshape(B, S, H, DQ)
    q_nope, q_pe = q[..., :DN], q[..., DN:]
    q_pe = apply_rope(q_pe, f64(freqs_cis))
    q_nope = silu(q_nope)
    q_pe = silu(q_pe)
    return q_nope * eta(q_nope)[:, None, :, None], q_pe * eta(q_pe)[:, None, :, None]


def e4m3fn_bytes(y):
    return np.clip(np.asarray(y, np.float64), -448.0, 448.0).astype(np.float32).astype(ml_dtypes.float8_e4m3fn).view(np.uint8)


def e4m3fn_values(b):
    return np.asarray(b, np.uint8).view(ml_dtypes.float8_e4m3fn).astype(np.float64)


def setup_inputs():
    d = draw0()
    x0 = np.asarray(d['x']).astype(np.float64)
    s = (np.max(np.abs(x0), axis=(0, 1), keepdims=True) / 448.0).astype(np.float32)
    out = {}
    for k, v in d.items():
        if k == 'x':
            out['x_bytes'] = e4m3fn_bytes(x0 / s.astype(np.float64))
            out['x_scale'] = s
        else:
            out[k] = v
    return out


def reference(x_bytes, x_scale, freqs_cis, wq_a_words, wq_a_scales, wq_b_words, wq_b_scales):
    return core(e4m3fn_values(x_bytes) * x_scale.astype(np.float64), freqs_cis, wq_a_words, wq_a_scales, wq_b_words, wq_b_scales)

@@ -1,0 +1,365 @@
+from contextlib import ExitStack
+
+import concourse.mybir as mybir
+from concourse.masks import make_identity
+
+F32 = mybir.dt.float32
+BF16 = mybir.dt.bfloat16
+U32 = mybir.dt.uint32
+I32 = mybir.dt.int32
+U8 = mybir.dt.uint8
+FP8 = mybir.dt.float8_e4m3fn
+FP8X4 = mybir.dt.float8_e4m3fn_x4
+FP4X4 = mybir.dt.float4_e2m1fn_x4
+ALU = mybir.AluOpType
+ACT = mybir.ActivationFunctionType
+AX = mybir.AxisListType
+
+B, S, D, H, J, QL = 4, 2048, 512, 4, 16, 512
+P = 128
+FLOPS = 2 * B * S * (D * QL + QL * H * 64)
+
+GROUPS = 4
+NU = B * GROUPS * 2
+
+
+def tile_ssa_pa_t_w4_kernel(tc, x_bytes, x_scale, freqs_cis, wq_a_words, wq_a_scales, wq_b_words, wq_b_scales, out_0, out_1):
+    nc = tc.nc
+    outs = (out_0, out_1)
+    with ExitStack() as ctx:
+        const = ctx.enter_context(tc.tile_pool(name="const", bufs=1))
+        xpool = ctx.enter_context(tc.tile_pool(name="xpool", bufs=B * GROUPS))
+        work = ctx.enter_context(tc.tile_pool(name="work", bufs=3))
+        res = ctx.enter_context(tc.tile_pool(name="res", bufs=3))
+        ps_t = ctx.enter_context(tc.psum_pool(name="ps_t", bufs=3))
+        ps_q = ctx.enter_context(tc.psum_pool(name="ps_q", bufs=2))
+        ps_n = ctx.enter_context(tc.psum_pool(name="ps_n", bufs=2))
+        ps_c = ctx.enter_context(tc.psum_pool(name="ps_c", bufs=1))
+        ctx.enter_context(tc.manual_schedule())
+
+        ident = const.tile([P, P], F32)
+        sc = const.tile([P, 4], F32)
+        wa_raw = const.tile([P, 1024], U8, align_bytes=64)
+        wsa_raw = const.tile([P, 512], U8, align_bytes=64)
+        wb_raw = const.tile([P, 512], U8, align_bytes=64)
+        wsb_raw = const.tile([P, 256], U8, align_bytes=64)
+        wa = const.tile([P, 1024], U8, align_bytes=64)
+        wsa = const.tile([P, 512], U8, align_bytes=64)
+        wbn = const.tile([P, 256], U8, align_bytes=64)
+        wbp = const.tile([P, 256], U8, align_bytes=64)
+        wsn = const.tile([P, 128], U8, align_bytes=64)
+        wsp = const.tile([P, 128], U8, align_bytes=64)
+        fr = const.tile([P, GROUPS, 4 * J * 2], BF16)
+        cd = const.tile([P, GROUPS, 4, 2, 2, H * J], F32)
+        warm = const.tile([P, 1], F32)
+        mxs = []
+        for b in range(B):
+            mx = const.tile([P, 2, P], F32, name="mx%d" % b)
+            mxs.append(mx)
+
+        nc.vector.memset(wsa_raw[:].bitcast(I32), 0)
+        nc.vector.memset(wsb_raw[:].bitcast(I32), 0)
+        nc.vector.memset(warm[:], 0.0)
+        nc.scalar.activation(warm[:], warm[:], func=ACT.Silu)
+
+        xr = []
+
+        def load_x(g, halves):
+            raw = xpool.tile([P, 2048], U8, name="xraw")
+            src = x_bytes[g // GROUPS, 512 * (g % GROUPS) : 512 * (g % GROUPS) + 512, :].rearrange("(p i) k -> p (i k)", i=4)
+            w = 2048 // halves
+            for h in range(halves):
+                nc.sync.dma_start(out=raw[:, h * w : (h + 1) * w], in_=src[:, h * w : (h + 1) * w])
+            xr.append(raw)
+
+        load_x(0, 2)
+        nc.sync.dma_start(out=sc[:], in_=x_scale.rearrange("a b (p t) -> p (a b t)", t=4))
+        nc.sync.dma_start(out=wa_raw[:], in_=wq_a_words[0])
+        for q in range(4):
+            nc.sync.dma_start(out=wsa_raw[32 * q : 32 * q + 4, :].bitcast(I32), in_=wq_a_scales[0, 4 * q : 4 * q + 4, :].bitcast(I32))
+        nc.sync.dma_start(out=fr[:], in_=freqs_cis.rearrange("(g p i) j c -> p g (i j c)", g=GROUPS, i=4))
+        nc.sync.dma_start(out=wb_raw[:], in_=wq_b_words[0])
+        for q in range(4):
+            nc.sync.dma_start(out=wsb_raw[32 * q : 32 * q + 4, :].bitcast(I32), in_=wq_b_scales[0, 4 * q : 4 * q + 4, :].bitcast(I32))
+        for g in range(1, B * GROUPS):
+            load_x(g, 1)
+
+        make_identity(nc, ident[:])
+        for g in range(GROUPS):
+            for e in range(2):
+                for k in range(2):
+                    cs = 0 if e == k else 1
+                    sign = -1.0 if (e == 1 and k == 0) else 1.0
+                    src = fr[:, g, :].rearrange("p (i j c) -> p i j c", j=J, c=2)[:, :, :, cs]
+                    nc.gpsimd.tensor_scalar(
+                        out=cd[:, g, :, e, k, :].rearrange("p i (h j) -> p i h j", h=H),
+                        in0=src.unsqueeze(2).to_broadcast([P, 4, H, J]),
+                        scalar1=sign, scalar2=0.0, op0=ALU.mult, op1=ALU.add,
+                    )
+            nc.gpsimd.memset(mxs[g][:], 0.0)
+
+        nc.vector.tensor_copy(
+            out=wa[:].rearrange("p (t m b) -> p t m b", t=4, b=2),
+            in_=wa_raw[:].rearrange("p (m t b) -> p t m b", t=4, b=2),
+        )
+        nc.vector.tensor_copy(
+            out=wsa[:].rearrange("p (t m) -> p t m", t=4),
+            in_=wsa_raw[:].rearrange("p (m t) -> p t m", t=4),
+        )
+
+        def prep_wb():
+            wv = wb_raw[:].rearrange("p (h k x) -> p h k x", h=H, k=2)
+            sv = wsb_raw[:].rearrange("p (h k x) -> p h k x", h=H, k=2)
+            nc.vector.tensor_copy(out=wbn[:].rearrange("p (h x) -> p h x", h=H), in_=wv[:, :, 0, :])
+            nc.vector.tensor_copy(out=wsn[:].rearrange("p (h x) -> p h x", h=H), in_=sv[:, :, 0, :])
+            for e in range(2):
+                nc.vector.tensor_copy(
+                    out=wbp[:, 128 * e : 128 * e + 128].rearrange("p (h j b) -> p h j b", h=H, b=2),
+                    in_=wv[:, :, 1, :].rearrange("p h (j e b) -> p h j e b", e=2, b=2)[:, :, :, e, :],
+                )
+                nc.vector.tensor_copy(
+                    out=wsp[:, 64 * e : 64 * e + 64].rearrange("p (h j) -> p h j", h=H),
+                    in_=sv[:, :, 1, :].rearrange("p h (j e) -> p h j e", e=2)[:, :, :, e],
+                )
+
+        st = {}
+
+        def cast(u):
+            xb = work.tile([P, 1024], BF16)
+            nc.scalar.copy(out=xb[:], in_=xr[u // 2][:, 1024 * (u % 2) : 1024 * (u % 2) + 1024].bitcast(FP8))
+            st["xb", u] = xb
+
+        def trans(u):
+            words = st["xb", u][:].bitcast(F32)
+            tp = ps_t.tile([P, 2, 2, P], F32)
+            for i in range(2):
+                for w in range(2):
+                    nc.tensor.transpose(tp[:, w, i, :], words[:, 256 * i + w : 256 * (i + 1) : 2], ident[:])
+            st["tp", u] = tp
+
+        def scale_x(u):
+            xg = work.tile([P, 1024], BF16, align_bytes=64)
+            nc.vector.tensor_tensor(
+                out=xg[:].rearrange("p (c u e) -> p c u e", u=2, e=2),
+                in0=st["tp", u][:].rearrange("p u i r -> p (u i r)").bitcast(BF16).rearrange("p (u c e) -> p c u e", u=2, e=2),
+                in1=sc[:].rearrange("p (o u e) -> p o u e", o=1, u=2).to_broadcast([P, 256, 2, 2]),
+                op=ALU.mult,
+            )
+            st["xg", u] = xg
+
+        def quant_x(u):
+            xq = work.tile([P, 256], U32, align_bytes=64)
+            xs = work.tile([P, 256], U8, align_bytes=64)
+            nc.vector.quantize_mx(out=xq[:].bitcast(FP8X4), scales=xs[:], in_=st["xg", u][:])
+            st["xq", u] = (xq, xs)
+
+        def mm1(u):
+            xq, xs = st["xq", u]
+            for i in range(2):
+                qc = ps_q.tile([P, 4, P], F32)
+                c = slice(128 * i, 128 * i + 128)
+                for t in range(4):
+                    nc.tensor.matmul_mx(
+                        out=qc[:, t, :],
+                        lhsT=wa[:, 256 * t : 256 * t + 256].bitcast(FP4X4), lhsT_scale=wsa[:, 128 * t : 128 * t + 128],
+                        rhs=xq[:, c].bitcast(FP8X4), rhs_scale=xs[:, c], start=True, stop=True,
+                    )
+                st["qc", u, i] = qc
+
+        def exit_q(u):
+            qg = work.tile([P, 1024], BF16, align_bytes=64)
+            for i in range(2):
+                nc.scalar.copy(
+                    out=qg[:, 512 * i : 512 * i + 512].rearrange("p (r t) -> p r t", t=4),
+                    in_=st["qc", u, i][:].rearrange("p t r -> p r t"),
+                )
+            st["qg", u] = qg
+
+        def quant_q(u):
+            qq = work.tile([P, 256], U32, align_bytes=64)
+            qs = work.tile([P, 256], U8, align_bytes=64)
+            nc.vector.quantize_mx(out=qq[:].bitcast(FP8X4), scales=qs[:], in_=st["qg", u][:])
+            st["qq", u] = (qq, qs)
+
+        def mm2(u):
+            qq, qs = st["qq", u]
+            nv = ps_n.tile([P, 4, P], F32)
+            for k, (w, s) in enumerate(((wbn, wsn), (wbp, wsp))):
+                for i in range(2):
+                    c = slice(128 * i, 128 * i + 128)
+                    nc.tensor.matmul_mx(
+                        out=nv[:, 2 * k + i, :],
+                        lhsT=qq[:, c].bitcast(FP8X4), lhsT_scale=qs[:, c],
+                        rhs=w[:].bitcast(FP4X4), rhs_scale=s[:], start=True, stop=True,
+                    )
+            st["np", u] = nv
+
+        def rope_mul(u):
+            g, hh = (u // 2) % GROUPS, u % 2
+            pt = work.tile([P, 4, 2, 64], F32)
+            nc.vector.tensor_tensor(
+                out=pt[:],
+                in0=st["np", u][:, 2:4, :].rearrange("p i (e x) -> p (i e) x", e=2).unsqueeze(2).to_broadcast([P, 4, 2, 64]),
+                in1=cd[:, g, 2 * hh : 2 * hh + 2, :, :, :].rearrange("p i e k x -> p (i e) k x"),
+                op=ALU.mult,
+            )
+            st["pt", u] = pt
+
+        def rope_add(u):
+            pr = work.tile([P, 2, P], F32)
+            v = st["pt", u][:].rearrange("p (i e) k x -> p i e (k x)", e=2)
+            nc.gpsimd.tensor_tensor(out=pr[:], in0=v[:, :, 0, :], in1=v[:, :, 1, :], op=ALU.add)
+            st["pr", u] = pr
+
+        def silu_n(u):
+            b, g, hh = u // 8, (u // 2) % GROUPS, u % 2
+            if u % 8 == 0:
+                ar = res.tile([P, 2, GROUPS, 512], F32)
+                st["ar", b] = ar
+            nc.scalar.activation(
+                st["ar", b][:, 0, g, 256 * hh : 256 * hh + 256],
+                st["np", u][:, 0:2, :].rearrange("p i x -> p (i x)"), func=ACT.Silu,
+            )
+
+        def silu_r(u):
+            b, g, hh = u // 8, (u // 2) % GROUPS, u % 2
+            nc.scalar.activation(
+                st["ar", b][:, 1, g, 256 * hh : 256 * hh + 256].rearrange("p (i x e) -> p i x e", i=2, e=2),
+                st["pr", u][:].rearrange("p i (e x) -> p i x e", e=2), func=ACT.Silu,
+            )
+
+        def row_max(u):
+            b, g, hh = u // 8, (u // 2) % GROUPS, u % 2
+            nc.vector.tensor_reduce(
+                out=mxs[b][:, hh, 2 * g : 2 * g + 2],
+                in_=st["ar", b][:, :, g, 256 * hh : 256 * hh + 256], axis=AX.X, op=ALU.max,
+            )
+
+        def eta_turn(b):
+            ct = ps_c.tile([P, 512], F32)
+            for hh in range(2):
+                nc.tensor.transpose(ct[:, 128 * hh : 128 * hh + 128], mxs[b][:, hh, :], ident[:])
+            st["ct", b] = ct
+
+        def eta_max(b, part=""):
+            m = const.tile([P, 4], F32, name="m%d%s" % (b, part))
+            st["m", b] = m
+            nc.vector.tensor_reduce(out=m[:, 0:1], in_=st["ct", b][:, 0:256], axis=AX.X, op=ALU.max)
+
+        def eta_nonzero(b):
+            m = st["m", b]
+            nc.vector.scalar_tensor_tensor(out=m[:, 1:2], in0=m[:, 0:1], scalar=0.0, in1=m[:, 0:1], op0=ALU.is_equal, op1=ALU.add)
+
+        def eta_recip(b):
+            m = st["m", b]
+            nc.vector.reciprocal(out=m[:, 2:3], in_=m[:, 1:2])
+
+        def eta_min(b):
+            m = st["m", b]
+            nc.vector.tensor_scalar(out=m[:, 3:4], in0=m[:, 2:3], scalar1=10.0, scalar2=1.0, op0=ALU.mult, op1=ALU.min)
+
+        def eta_spread(b):
+            ce = ps_c.tile([P, 512], F32, name="ct")
+            nc.tensor.transpose(ce[:, 0:128], st["m", b][:, 3:4].to_broadcast([P, P]), ident[:])
+            st["ce", b] = ce
+
+        def eta_out(b, eng, part=""):
+            eb = const.tile([P, 8], F32, name="eb%d%s" % (b, part))
+            if eng == "s":
+                nc.scalar.copy(out=eb[:], in_=st["ce", b][:, 0:8])
+            else:
+                nc.vector.tensor_copy(out=eb[:], in_=st["ce", b][:, 0:8])
+            st["eb", b] = eb
+
+        def clamp(b, g, k, eng):
+            v = st["ar", b][:, k, g, :].rearrange("p (i h d) -> p i h d", i=4, h=H)
+            for h in range(H):
+                e = st["eb", b][:, 2 * h + k : 2 * h + k + 1]
+                eng.tensor_scalar(out=v[:, :, h, :], in0=v[:, :, h, :], scalar1=e, scalar2=0.0, op0=ALU.mult, op1=ALU.add)
+            nc.sync.dma_start(
+                out=outs[k][b, 512 * g : 512 * g + 512, :, :].rearrange("(p i) h d -> p (i h d)", i=4),
+                in_=st["ar", b][:, k, g, :],
+            )
+
+        def on(u):
+            return 0 <= u < NU
+
+        for u in range(-2, NU + 3):
+            b0, r0 = divmod(u - 11, 8)
+            eta_b = b0 if (r0 == 0 and 0 <= b0 < B - 1) else None
+            if u == NU + 1:
+                eta_b = B - 1
+            b1, r1 = divmod(u - 12, 8)
+            if on(u - 2):
+                quant_q(u - 2)
+                mm2(u - 2)
+            if eta_b is not None:
+                eta_max(eta_b)
+            if on(u - 1):
+                exit_q(u - 1)
+            if on(u):
+                scale_x(u)
+            if eta_b is not None:
+                eta_nonzero(eta_b)
+            if on(u - 3):
+                silu_r(u - 3)
+            if r1 == 0 and 0 <= b1 < B - 1:
+                eta_out(b1, "s")
+            if u == NU + 2:
+                eta_out(B - 1, "s")
+            if on(u + 2):
+                cast(u + 2)
+            if on(u + 1):
+                trans(u + 1)
+            if on(u - 2):
+                rope_mul(u - 2)
+                silu_n(u - 2)
+                rope_add(u - 2)
+            if eta_b is not None:
+                eta_recip(eta_b)
+            if on(u):
+                quant_x(u)
+                mm1(u)
+            if u == 0:
+                prep_wb()
+            if on(u - 3):
+                row_max(u - 3)
+            if eta_b is not None:
+                eta_min(eta_b)
+                eta_spread(eta_b)
+            if 0 <= b1 < B - 1:
+                clamp(b1, r1 // 2, r1 % 2, nc.gpsimd)
+            bt, rt = divmod(u - 10, 8)
+            if rt == 0 and 0 <= bt < B:
+                eta_turn(bt)
+            if u == NU:
+                eta_turn(B - 1)
+        b = B - 1
+        last = st["ar", b]
+        for r1 in range(NU + 3 - 12 - 8 * (B - 2), 8):
+            clamp(B - 2, r1 // 2, r1 % 2, nc.gpsimd)
+        for k in range(2):
+            v = last[:, k, 0:3, :].rearrange("p g (i h d) -> p (g i) h d", i=4, h=H)
+            for h in range(3):
+                nc.gpsimd.tensor_scalar(
+                    out=v[:, :, h, :], in0=v[:, :, h, :], scalar1=st["eb", b][:, 2 * h + k : 2 * h + k + 1], scalar2=0.0, op0=ALU.mult, op1=ALU.add
+                )
+        for k in range(2):
+            v = last[:, k, 3, :].rearrange("p (i h d) -> p i h d", i=4, h=H)
+            for h in range(3):
+                nc.scalar.activation(v[:, :, h, :], v[:, :, h, :], func=ACT.Copy, scale=st["eb", b][:, 2 * h + k : 2 * h + k + 1])
+        eta_max(b, "z")
+        eta_nonzero(b)
+        eta_recip(b)
+        eta_min(b)
+        eta_spread(b)
+        eta_out(b, "v", "z")
+        for k in range(2):
+            v = last[:, k, :, :].rearrange("p g (i h d) -> p (g i) h d", i=4, h=H)[:, :, 3, :]
+            nc.vector.tensor_scalar(out=v, in0=v, scalar1=st["eb", b][:, 6 + k : 7 + k], scalar2=None, op0=ALU.mult)
+            eng = nc.sync if k == 0 else nc.scalar
+            for g in range(GROUPS):
+                eng.dma_start(
+                    out=outs[k][b, 512 * g : 512 * g + 512, :, :].rearrange("(p i) h d -> p (i h d)", i=4),
+                    in_=last[:, k, g, :],
+                )

@@ -31,8 +31,8 @@ def tile_ssa_pa_t_w4_kernel(tc, x_bytes, x_scale, freqs_cis, wq_a_words, wq_a_sc
         xpool = ctx.enter_context(tc.tile_pool(name="xpool", bufs=B * GROUPS))
         work = ctx.enter_context(tc.tile_pool(name="work", bufs=3))
         res = ctx.enter_context(tc.tile_pool(name="res", bufs=3))
-        ps_t = ctx.enter_context(tc.psum_pool(name="ps_t", bufs=3))
-        ps_q = ctx.enter_context(tc.psum_pool(name="ps_q", bufs=2))
+        ps_t = ctx.enter_context(tc.psum_pool(name="ps_t", bufs=2))
+        ps_q = ctx.enter_context(tc.psum_pool(name="ps_q", bufs=3))
         ps_n = ctx.enter_context(tc.psum_pool(name="ps_n", bufs=2))
         ps_c = ctx.enter_context(tc.psum_pool(name="ps_c", bufs=1))
         ctx.enter_context(tc.manual_schedule())
@@ -271,79 +271,86 @@ def tile_ssa_pa_t_w4_kernel(tc, x_bytes, x_scale, freqs_cis, wq_a_words, wq_a_sc
                 nc.vector.tensor_copy(out=eb[:], in_=st["ce", b][:, 0:8])
             st["eb", b] = eb
 
-        def clamp(b, g, k, eng):
-            v = st["ar", b][:, k, g, :].rearrange("p (i h d) -> p i h d", i=4, h=H)
-            for h in range(H):
-                e = st["eb", b][:, 2 * h + k : 2 * h + k + 1]
-                eng.tensor_scalar(out=v[:, :, h, :], in0=v[:, :, h, :], scalar1=e, scalar2=0.0, op0=ALU.mult, op1=ALU.add)
-            nc.sync.dma_start(
+        def clamp(b, step):
+            k, gp, h0 = (step // 2) % 2, step // 4, 2 * (step % 2)
+            v = st["ar", b][:, k, 2 * gp : 2 * gp + 2, :].rearrange("p g (i h d) -> p (g i) h d", i=4, h=H)
+            for h in range(h0, h0 + 2):
+                nc.gpsimd.tensor_scalar(
+                    out=v[:, :, h, :], in0=v[:, :, h, :], scalar1=st["eb", b][:, 2 * h + k : 2 * h + k + 1], scalar2=0.0, op0=ALU.mult, op1=ALU.add
+                )
+            if h0 == 2:
+                for g in range(2 * gp, 2 * gp + 2):
+                    store(b, g, k, nc.sync)
+
+        def store(b, g, k, eng):
+            eng.dma_start(
                 out=outs[k][b, 512 * g : 512 * g + 512, :, :].rearrange("(p i) h d -> p (i h d)", i=4),
                 in_=st["ar", b][:, k, g, :],
             )
 
+        def last_early():
+            b = B - 1
+            for k, eng in ((0, nc.vector), (1, nc.gpsimd)):
+                v = st["ar", b][:, k, 0:3, :].rearrange("p g (i h d) -> p (g i) h d", i=4, h=H)
+                for h in range(3):
+                    eng.tensor_scalar(
+                        out=v[:, :, h, :], in0=v[:, :, h, :], scalar1=st["eb", b][:, 2 * h + k : 2 * h + k + 1], scalar2=0.0, op0=ALU.mult, op1=ALU.add
+                    )
+
         def on(u):
             return 0 <= u < NU
 
-        for u in range(-2, NU + 3):
-            b0, r0 = divmod(u - 11, 8)
+        for u in range(-2, NU + 6):
+            b0, r0 = divmod(u - 14, 8)
             eta_b = b0 if (r0 == 0 and 0 <= b0 < B - 1) else None
-            if u == NU + 1:
+            if u == NU + 4:
                 eta_b = B - 1
-            b1, r1 = divmod(u - 12, 8)
-            if on(u - 2):
-                quant_q(u - 2)
-                mm2(u - 2)
+            b1, r1 = divmod(u - 15, 8)
+            if on(u - 3):
+                quant_q(u - 3)
+                mm2(u - 3)
             if eta_b is not None:
                 eta_max(eta_b)
             if on(u - 1):
-                exit_q(u - 1)
-            if on(u):
-                scale_x(u)
+                quant_x(u - 1)
+                mm1(u - 1)
+            if on(u - 2):
+                exit_q(u - 2)
+            if on(u - 4):
+                rope_mul(u - 4)
+                silu_n(u - 4)
+                rope_add(u - 4)
+            if (r1 == 0 and 0 <= b1 < B - 1) or u == NU + 5:
+                eta_out(b1 if u < NU + 5 else B - 1, "s")
+            if on(u - 5):
+                silu_r(u - 5)
             if eta_b is not None:
                 eta_nonzero(eta_b)
-            if on(u - 3):
-                silu_r(u - 3)
-            if r1 == 0 and 0 <= b1 < B - 1:
-                eta_out(b1, "s")
-            if u == NU + 2:
-                eta_out(B - 1, "s")
+            if u == NU + 5:
+                last_early()
+            if on(u - 6):
+                row_max(u - 6)
             if on(u + 2):
                 cast(u + 2)
             if on(u + 1):
                 trans(u + 1)
-            if on(u - 2):
-                rope_mul(u - 2)
-                silu_n(u - 2)
-                rope_add(u - 2)
             if eta_b is not None:
                 eta_recip(eta_b)
             if on(u):
-                quant_x(u)
-                mm1(u)
+                scale_x(u)
             if u == 0:
                 prep_wb()
-            if on(u - 3):
-                row_max(u - 3)
             if eta_b is not None:
                 eta_min(eta_b)
                 eta_spread(eta_b)
             if 0 <= b1 < B - 1:
-                clamp(b1, r1 // 2, r1 % 2, nc.gpsimd)
-            bt, rt = divmod(u - 10, 8)
-            if rt == 0 and 0 <= bt < B:
-                eta_turn(bt)
-            if u == NU:
-                eta_turn(B - 1)
+                clamp(b1, r1)
+            bt, rt = divmod(u - 13, 8)
+            if (rt == 0 and 0 <= bt < B) or u == NU + 3:
+                eta_turn(bt if u != NU + 3 else B - 1)
         b = B - 1
         last = st["ar", b]
-        for r1 in range(NU + 3 - 12 - 8 * (B - 2), 8):
-            clamp(B - 2, r1 // 2, r1 % 2, nc.gpsimd)
-        for k in range(2):
-            v = last[:, k, 0:3, :].rearrange("p g (i h d) -> p (g i) h d", i=4, h=H)
-            for h in range(3):
-                nc.gpsimd.tensor_scalar(
-                    out=v[:, :, h, :], in0=v[:, :, h, :], scalar1=st["eb", b][:, 2 * h + k : 2 * h + k + 1], scalar2=0.0, op0=ALU.mult, op1=ALU.add
-                )
+        clamp(b - 1, 7)
         for k in range(2):
             v = last[:, k, 3, :].rearrange("p (i h d) -> p i h d", i=4, h=H)
             for h in range(3):
@@ -357,9 +364,5 @@ def tile_ssa_pa_t_w4_kernel(tc, x_bytes, x_scale, freqs_cis, wq_a_words, wq_a_sc
         for k in range(2):
             v = last[:, k, :, :].rearrange("p g (i h d) -> p (g i) h d", i=4, h=H)[:, :, 3, :]
             nc.vector.tensor_scalar(out=v, in0=v, scalar1=st["eb", b][:, 6 + k : 7 + k], scalar2=None, op0=ALU.mult)
-            eng = nc.sync if k == 0 else nc.scalar
             for g in range(GROUPS):
-                eng.dma_start(
-                    out=outs[k][b, 512 * g : 512 * g + 512, :, :].rearrange("(p i) h d -> p (i h d)", i=4),
-                    in_=last[:, k, g, :],
-                )
+                store(b, g, k, nc.sync if k == 0 else nc.scalar)

@@ -125,7 +125,7 @@ def tile_ssa_pa_t_w4_kernel(tc, x_bytes, x_scale, freqs_cis, wq_a_words, wq_a_sc
         st = {}
 
         def cast(u):
-            xb = work.tile([P, 1024], BF16)
+            xb = work.tile([P, 1024], BF16, bufs=6)
             nc.scalar.copy(out=xb[:], in_=xr[u // 2][:, 1024 * (u % 2) : 1024 * (u % 2) + 1024].bitcast(FP8))
             st["xb", u] = xb
 
@@ -165,6 +165,10 @@ def tile_ssa_pa_t_w4_kernel(tc, x_bytes, x_scale, freqs_cis, wq_a_words, wq_a_sc
                         rhs=xq[:, c].bitcast(FP8X4), rhs_scale=xs[:, c], start=True, stop=True,
                     )
                 st["qc", u, i] = qc
+
+        def keep_busy(u):
+            ct = ps_c.tile([P, 512], F32)
+            nc.tensor.matmul(ct[:], lhsT=st["xb", u][:, 0:128], rhs=st["xb", u][:, 0:512], start=True, stop=True)
 
         def exit_q(u):
             qg = work.tile([P, 1024], BF16, align_bytes=64)
@@ -300,12 +304,14 @@ def tile_ssa_pa_t_w4_kernel(tc, x_bytes, x_scale, freqs_cis, wq_a_words, wq_a_sc
         def on(u):
             return 0 <= u < NU
 
-        for u in range(-2, NU + 6):
+        for u in range(-3, NU + 6):
             b0, r0 = divmod(u - 14, 8)
             eta_b = b0 if (r0 == 0 and 0 <= b0 < B - 1) else None
             if u == NU + 4:
                 eta_b = B - 1
             b1, r1 = divmod(u - 15, 8)
+            if on(u + 1):
+                trans(u + 1)
             if on(u - 3):
                 quant_q(u - 3)
                 mm2(u - 3)
@@ -314,6 +320,7 @@ def tile_ssa_pa_t_w4_kernel(tc, x_bytes, x_scale, freqs_cis, wq_a_words, wq_a_sc
             if on(u - 1):
                 quant_x(u - 1)
                 mm1(u - 1)
+                keep_busy(u - 1)
             if on(u - 2):
                 exit_q(u - 2)
             if on(u - 4):
@@ -330,10 +337,8 @@ def tile_ssa_pa_t_w4_kernel(tc, x_bytes, x_scale, freqs_cis, wq_a_words, wq_a_sc
                 last_early()
             if on(u - 6):
                 row_max(u - 6)
-            if on(u + 2):
-                cast(u + 2)
-            if on(u + 1):
-                trans(u + 1)
+            if on(u + 3):
+                cast(u + 3)
             if eta_b is not None:
                 eta_recip(eta_b)
             if on(u):

@@ -64,25 +64,25 @@ def tile_ssa_pa_t_w4_kernel(tc, x_bytes, x_scale, freqs_cis, wq_a_words, wq_a_sc
 
         xr = []
 
-        def load_x(g, halves):
-            raw = xpool.tile([P, 2048], U8, name="xraw")
+        def load_x(g, cols):
+            if g == len(xr):
+                xraw = xpool.tile([P, 2048], U8)
+                xr.append(xraw)
             src = x_bytes[g // GROUPS, 512 * (g % GROUPS) : 512 * (g % GROUPS) + 512, :].rearrange("(p i) k -> p (i k)", i=4)
-            w = 2048 // halves
-            for h in range(halves):
-                nc.sync.dma_start(out=raw[:, h * w : (h + 1) * w], in_=src[:, h * w : (h + 1) * w])
-            xr.append(raw)
+            nc.sync.dma_start(out=xr[g][:, cols], in_=src[:, cols])
 
-        load_x(0, 2)
+        load_x(0, slice(0, 1024))
         nc.sync.dma_start(out=sc[:], in_=x_scale.rearrange("a b (p t) -> p (a b t)", t=4))
         nc.sync.dma_start(out=wa_raw[:], in_=wq_a_words[0])
+        nc.sync.dma_start(out=wb_raw[:], in_=wq_b_words[0])
+        load_x(0, slice(1024, 2048))
         for q in range(4):
             nc.sync.dma_start(out=wsa_raw[32 * q : 32 * q + 4, :].bitcast(I32), in_=wq_a_scales[0, 4 * q : 4 * q + 4, :].bitcast(I32))
         nc.sync.dma_start(out=fr[:], in_=freqs_cis.rearrange("(g p i) j c -> p g (i j c)", g=GROUPS, i=4))
-        nc.sync.dma_start(out=wb_raw[:], in_=wq_b_words[0])
         for q in range(4):
             nc.sync.dma_start(out=wsb_raw[32 * q : 32 * q + 4, :].bitcast(I32), in_=wq_b_scales[0, 4 * q : 4 * q + 4, :].bitcast(I32))
         for g in range(1, B * GROUPS):
-            load_x(g, 1)
+            load_x(g, slice(0, 2048))
 
         make_identity(nc, ident[:])
         for g in range(GROUPS):
@@ -96,27 +96,25 @@ def tile_ssa_pa_t_w4_kernel(tc, x_bytes, x_scale, freqs_cis, wq_a_words, wq_a_sc
                         in0=src.unsqueeze(2).to_broadcast([P, 4, H, J]),
                         scalar1=sign, scalar2=0.0, op0=ALU.mult, op1=ALU.add,
                     )
-            nc.gpsimd.memset(mxs[g][:], 0.0)
+        for b in range(B):
+            nc.gpsimd.memset(mxs[b][:], 0.0)
 
         nc.vector.tensor_copy(
             out=wa[:].rearrange("p (t m b) -> p t m b", t=4, b=2),
             in_=wa_raw[:].rearrange("p (m t b) -> p t m b", t=4, b=2),
         )
-        nc.vector.tensor_copy(
-            out=wsa[:].rearrange("p (t m) -> p t m", t=4),
-            in_=wsa_raw[:].rearrange("p (m t) -> p t m", t=4),
-        )
+        wv = wb_raw[:].rearrange("p (h k x) -> p h k x", h=H, k=2)
+        nc.vector.tensor_copy(out=wbn[:].rearrange("p (h x) -> p h x", h=H), in_=wv[:, :, 0, :])
+        for e in range(2):
+            nc.vector.tensor_copy(
+                out=wbp[:, 128 * e : 128 * e + 128].rearrange("p (h j b) -> p h j b", h=H, b=2),
+                in_=wv[:, :, 1, :].rearrange("p h (j e b) -> p h j e b", e=2, b=2)[:, :, :, e, :],
+            )
 
-        def prep_wb():
-            wv = wb_raw[:].rearrange("p (h k x) -> p h k x", h=H, k=2)
+        def scales_of_b():
             sv = wsb_raw[:].rearrange("p (h k x) -> p h k x", h=H, k=2)
-            nc.vector.tensor_copy(out=wbn[:].rearrange("p (h x) -> p h x", h=H), in_=wv[:, :, 0, :])
             nc.vector.tensor_copy(out=wsn[:].rearrange("p (h x) -> p h x", h=H), in_=sv[:, :, 0, :])
             for e in range(2):
-                nc.vector.tensor_copy(
-                    out=wbp[:, 128 * e : 128 * e + 128].rearrange("p (h j b) -> p h j b", h=H, b=2),
-                    in_=wv[:, :, 1, :].rearrange("p h (j e b) -> p h j e b", e=2, b=2)[:, :, :, e, :],
-                )
                 nc.vector.tensor_copy(
                     out=wsp[:, 64 * e : 64 * e + 64].rearrange("p (h j) -> p h j", h=H),
                     in_=sv[:, :, 1, :].rearrange("p h (j e) -> p h j e", e=2)[:, :, :, e],
@@ -245,8 +243,8 @@ def tile_ssa_pa_t_w4_kernel(tc, x_bytes, x_scale, freqs_cis, wq_a_words, wq_a_sc
                 nc.tensor.transpose(ct[:, 128 * hh : 128 * hh + 128], mxs[b][:, hh, :], ident[:])
             st["ct", b] = ct
 
-        def eta_max(b, part=""):
-            m = const.tile([P, 4], F32, name="m%d%s" % (b, part))
+        def eta_max(b):
+            m = const.tile([P, 4], F32, name="m%d" % b)
             st["m", b] = m
             nc.vector.tensor_reduce(out=m[:, 0:1], in_=st["ct", b][:, 0:256], axis=AX.X, op=ALU.max)
 
@@ -267,23 +265,18 @@ def tile_ssa_pa_t_w4_kernel(tc, x_bytes, x_scale, freqs_cis, wq_a_words, wq_a_sc
             nc.tensor.transpose(ce[:, 0:128], st["m", b][:, 3:4].to_broadcast([P, P]), ident[:])
             st["ce", b] = ce
 
-        def eta_out(b, eng, part=""):
-            eb = const.tile([P, 8], F32, name="eb%d%s" % (b, part))
-            if eng == "s":
-                nc.scalar.copy(out=eb[:], in_=st["ce", b][:, 0:8])
-            else:
-                nc.vector.tensor_copy(out=eb[:], in_=st["ce", b][:, 0:8])
+        def eta_out(b):
+            eb = const.tile([P, 8], F32, name="eb%d" % b)
+            nc.scalar.copy(out=eb[:], in_=st["ce", b][:, 0:8])
             st["eb", b] = eb
 
         def clamp(b, step):
-            k, gp, h0 = (step // 2) % 2, step // 4, 2 * (step % 2)
-            v = st["ar", b][:, k, 2 * gp : 2 * gp + 2, :].rearrange("p g (i h d) -> p (g i) h d", i=4, h=H)
-            for h in range(h0, h0 + 2):
-                nc.gpsimd.tensor_scalar(
-                    out=v[:, :, h, :], in0=v[:, :, h, :], scalar1=st["eb", b][:, 2 * h + k : 2 * h + k + 1], scalar2=0.0, op0=ALU.mult, op1=ALU.add
-                )
-            if h0 == 2:
-                for g in range(2 * gp, 2 * gp + 2):
+            h, k = step % 4, step // 4
+            v = st["ar", b][:, k, :, :].rearrange("p g (i h d) -> p (g i) h d", i=4, h=H)[:, :, h, :]
+            e = st["eb", b][:, 2 * h + k : 2 * h + k + 1]
+            nc.gpsimd.tensor_scalar(out=v, in0=v, scalar1=e, scalar2=0.0, op0=ALU.mult, op1=ALU.add)
+            if h == H - 1:
+                for g in range(GROUPS):
                     store(b, g, k, nc.sync)
 
         def store(b, g, k, eng):
@@ -292,14 +285,16 @@ def tile_ssa_pa_t_w4_kernel(tc, x_bytes, x_scale, freqs_cis, wq_a_words, wq_a_sc
                 in_=st["ar", b][:, k, g, :],
             )
 
-        def last_early():
+        def last_early(groups):
             b = B - 1
-            for k, eng in ((0, nc.vector), (1, nc.gpsimd)):
-                v = st["ar", b][:, k, 0:3, :].rearrange("p g (i h d) -> p (g i) h d", i=4, h=H)
+            for k in range(2):
+                v = st["ar", b][:, k, groups, :].rearrange("p g (i h d) -> p (g i) h d", i=4, h=H)
                 for h in range(3):
-                    eng.tensor_scalar(
-                        out=v[:, :, h, :], in0=v[:, :, h, :], scalar1=st["eb", b][:, 2 * h + k : 2 * h + k + 1], scalar2=0.0, op0=ALU.mult, op1=ALU.add
-                    )
+                    w, e = v[:, :, h, :], st["eb", b][:, 2 * h + k : 2 * h + k + 1]
+                    if k == 0:
+                        nc.scalar.activation(w, w, func=ACT.Copy, scale=e)
+                    else:
+                        nc.gpsimd.tensor_scalar(out=w, in0=w, scalar1=e, scalar2=0.0, op0=ALU.mult, op1=ALU.add)
 
         def on(u):
             return 0 <= u < NU
@@ -310,6 +305,8 @@ def tile_ssa_pa_t_w4_kernel(tc, x_bytes, x_scale, freqs_cis, wq_a_words, wq_a_sc
             if u == NU + 4:
                 eta_b = B - 1
             b1, r1 = divmod(u - 15, 8)
+            if (r1 == 0 and 0 <= b1 < B - 1) or u == NU + 5:
+                eta_out(b1 if u < NU + 5 else B - 1)
             if on(u + 1):
                 trans(u + 1)
             if on(u - 3):
@@ -327,14 +324,12 @@ def tile_ssa_pa_t_w4_kernel(tc, x_bytes, x_scale, freqs_cis, wq_a_words, wq_a_sc
                 rope_mul(u - 4)
                 silu_n(u - 4)
                 rope_add(u - 4)
-            if (r1 == 0 and 0 <= b1 < B - 1) or u == NU + 5:
-                eta_out(b1 if u < NU + 5 else B - 1, "s")
             if on(u - 5):
                 silu_r(u - 5)
             if eta_b is not None:
                 eta_nonzero(eta_b)
             if u == NU + 5:
-                last_early()
+                last_early(slice(0, 3))
             if on(u - 6):
                 row_max(u - 6)
             if on(u + 3):
@@ -344,30 +339,35 @@ def tile_ssa_pa_t_w4_kernel(tc, x_bytes, x_scale, freqs_cis, wq_a_words, wq_a_sc
             if on(u):
                 scale_x(u)
             if u == 0:
-                prep_wb()
+                nc.vector.tensor_copy(
+                    out=wsa[:].rearrange("p (t m) -> p t m", t=4),
+                    in_=wsa_raw[:].rearrange("p (m t) -> p t m", t=4),
+                )
+            if u == 1:
+                scales_of_b()
             if eta_b is not None:
                 eta_min(eta_b)
                 eta_spread(eta_b)
             if 0 <= b1 < B - 1:
                 clamp(b1, r1)
             bt, rt = divmod(u - 13, 8)
-            if (rt == 0 and 0 <= bt < B) or u == NU + 3:
+            if (rt == 0 and 0 <= bt < B - 1) or u == NU + 3:
                 eta_turn(bt if u != NU + 3 else B - 1)
         b = B - 1
-        last = st["ar", b]
         clamp(b - 1, 7)
+        last_early(slice(3, 4))
+        cl = ps_c.tile([P, 2, 2, P], F32, name="ct")
         for k in range(2):
-            v = last[:, k, 3, :].rearrange("p (i h d) -> p i h d", i=4, h=H)
-            for h in range(3):
-                nc.scalar.activation(v[:, :, h, :], v[:, :, h, :], func=ACT.Copy, scale=st["eb", b][:, 2 * h + k : 2 * h + k + 1])
-        eta_max(b, "z")
-        eta_nonzero(b)
-        eta_recip(b)
-        eta_min(b)
-        eta_spread(b)
-        eta_out(b, "v", "z")
+            for hh in range(2):
+                nc.tensor.transpose(cl[:, k, hh, :], mxs[b][:, hh, 6 + k : 7 + k].to_broadcast([P, P]), ident[:])
+        ml = const.tile([P, 4, 2], F32)
+        nc.vector.tensor_reduce(out=ml[:, 0, :], in_=cl[:].rearrange("p k h r -> p k (h r)"), axis=AX.X, op=ALU.max)
+        nc.vector.scalar_tensor_tensor(out=ml[:, 1, :], in0=ml[:, 0, :], scalar=0.0, in1=ml[:, 0, :], op0=ALU.is_equal, op1=ALU.add)
+        nc.vector.reciprocal(out=ml[:, 2, :], in_=ml[:, 1, :])
+        nc.vector.tensor_scalar(out=ml[:, 3, :], in0=ml[:, 2, :], scalar1=10.0, scalar2=1.0, op0=ALU.mult, op1=ALU.min)
         for k in range(2):
-            v = last[:, k, :, :].rearrange("p g (i h d) -> p (g i) h d", i=4, h=H)[:, :, 3, :]
-            nc.vector.tensor_scalar(out=v, in0=v, scalar1=st["eb", b][:, 6 + k : 7 + k], scalar2=None, op0=ALU.mult)
-            for g in range(GROUPS):
-                store(b, g, k, nc.sync if k == 0 else nc.scalar)
+            for gp in range(2):
+                v = st["ar", b][:, k, 2 * gp : 2 * gp + 2, :].rearrange("p g (i h d) -> p (g i) h d", i=4, h=H)[:, :, 3, :]
+                nc.vector.tensor_scalar(out=v, in0=v, scalar1=ml[:, 3, k : k + 1], scalar2=None, op0=ALU.mult)
+                for g in range(2 * gp, 2 * gp + 2):
+                    store(b, g, k, nc.sync if k == 0 else nc.scalar)

@@ -124,7 +124,9 @@ def tile_ssa_pa_t_w4_kernel(tc, x_bytes, x_scale, freqs_cis, wq_a_words, wq_a_sc
 
         def cast(u):
             xb = work.tile([P, 1024], BF16, bufs=6)
-            nc.scalar.copy(out=xb[:], in_=xr[u // 2][:, 1024 * (u % 2) : 1024 * (u % 2) + 1024].bitcast(FP8))
+            w = 512 if u == 0 else 1024
+            for c in range(0, 1024, w):
+                nc.scalar.copy(out=xb[:, c : c + w], in_=xr[u // 2][:, 1024 * (u % 2) + c : 1024 * (u % 2) + c + w].bitcast(FP8))
             st["xb", u] = xb
 
         def trans(u):
@@ -196,16 +198,18 @@ def tile_ssa_pa_t_w4_kernel(tc, x_bytes, x_scale, freqs_cis, wq_a_words, wq_a_sc
                     )
             st["np", u] = nv
 
-        def rope_mul(u):
+        def rope_mul(u, blocks):
             g, hh = (u // 2) % GROUPS, u % 2
-            pt = work.tile([P, 4, 2, 64], F32)
+            if blocks.start == 0:
+                pt = work.tile([P, 4, 2, 64], F32)
+                st["pt", u] = pt
+            n = blocks.stop - blocks.start
             nc.vector.tensor_tensor(
-                out=pt[:],
-                in0=st["np", u][:, 2:4, :].rearrange("p i (e x) -> p (i e) x", e=2).unsqueeze(2).to_broadcast([P, 4, 2, 64]),
-                in1=cd[:, g, 2 * hh : 2 * hh + 2, :, :, :].rearrange("p i e k x -> p (i e) k x"),
+                out=st["pt", u][:, blocks],
+                in0=st["np", u][:, 2:4, :].rearrange("p i (e x) -> p (i e) x", e=2)[:, blocks].unsqueeze(2).to_broadcast([P, n, 2, 64]),
+                in1=cd[:, g, 2 * hh : 2 * hh + 2, :, :, :].rearrange("p i e k x -> p (i e) k x")[:, blocks],
                 op=ALU.mult,
             )
-            st["pt", u] = pt
 
         def rope_add(u):
             pr = work.tile([P, 2, P], F32)
@@ -230,11 +234,11 @@ def tile_ssa_pa_t_w4_kernel(tc, x_bytes, x_scale, freqs_cis, wq_a_words, wq_a_sc
                 st["pr", u][:].rearrange("p i (e x) -> p i x e", e=2), func=ACT.Silu,
             )
 
-        def row_max(u):
+        def row_max(u, kinds):
             b, g, hh = u // 8, (u // 2) % GROUPS, u % 2
             nc.vector.tensor_reduce(
-                out=mxs[b][:, hh, 2 * g : 2 * g + 2],
-                in_=st["ar", b][:, :, g, 256 * hh : 256 * hh + 256], axis=AX.X, op=ALU.max,
+                out=mxs[b][:, hh, 2 * g + kinds.start : 2 * g + kinds.stop],
+                in_=st["ar", b][:, kinds, g, 256 * hh : 256 * hh + 256], axis=AX.X, op=ALU.max,
             )
 
         def eta_turn(b):
@@ -285,16 +289,17 @@ def tile_ssa_pa_t_w4_kernel(tc, x_bytes, x_scale, freqs_cis, wq_a_words, wq_a_sc
                 in_=st["ar", b][:, k, g, :],
             )
 
-        def last_early(groups):
+        def last_early(k, groups, eng):
             b = B - 1
-            for k in range(2):
-                v = st["ar", b][:, k, groups, :].rearrange("p g (i h d) -> p (g i) h d", i=4, h=H)
-                for h in range(3):
-                    w, e = v[:, :, h, :], st["eb", b][:, 2 * h + k : 2 * h + k + 1]
-                    if k == 0:
-                        nc.scalar.activation(w, w, func=ACT.Copy, scale=e)
-                    else:
-                        nc.gpsimd.tensor_scalar(out=w, in0=w, scalar1=e, scalar2=0.0, op0=ALU.mult, op1=ALU.add)
+            v = st["ar", b][:, k, groups, :].rearrange("p g (i h d) -> p (g i) h d", i=4, h=H)
+            for h in range(3):
+                w, e = v[:, :, h, :], st["eb", b][:, 2 * h + k : 2 * h + k + 1]
+                if eng == "s":
+                    nc.scalar.activation(w, w, func=ACT.Copy, scale=e)
+                elif eng == "g":
+                    nc.gpsimd.tensor_scalar(out=w, in0=w, scalar1=e, scalar2=0.0, op0=ALU.mult, op1=ALU.add)
+                else:
+                    nc.vector.tensor_scalar(out=w, in0=w, scalar1=e, scalar2=None, op0=ALU.mult)
 
         def on(u):
             return 0 <= u < NU
@@ -309,6 +314,8 @@ def tile_ssa_pa_t_w4_kernel(tc, x_bytes, x_scale, freqs_cis, wq_a_words, wq_a_sc
                 eta_out(b1 if u < NU + 5 else B - 1)
             if on(u + 1):
                 trans(u + 1)
+            if on(u - 4):
+                rope_mul(u - 4, slice(0, 3))
             if on(u - 3):
                 quant_q(u - 3)
                 mm2(u - 3)
@@ -321,7 +328,7 @@ def tile_ssa_pa_t_w4_kernel(tc, x_bytes, x_scale, freqs_cis, wq_a_words, wq_a_sc
             if on(u - 2):
                 exit_q(u - 2)
             if on(u - 4):
-                rope_mul(u - 4)
+                rope_mul(u - 4, slice(3, 4))
                 silu_n(u - 4)
                 rope_add(u - 4)
             if on(u - 5):
@@ -329,9 +336,10 @@ def tile_ssa_pa_t_w4_kernel(tc, x_bytes, x_scale, freqs_cis, wq_a_words, wq_a_sc
             if eta_b is not None:
                 eta_nonzero(eta_b)
             if u == NU + 5:
-                last_early(slice(0, 3))
-            if on(u - 6):
-                row_max(u - 6)
+                last_early(0, slice(0, 3), "s")
+                last_early(1, slice(0, 3), "g")
+            if on(u - 6) and u - 6 < NU - 1:
+                row_max(u - 6, slice(0, 2))
             if on(u + 3):
                 cast(u + 3)
             if eta_b is not None:
@@ -355,19 +363,46 @@ def tile_ssa_pa_t_w4_kernel(tc, x_bytes, x_scale, freqs_cis, wq_a_words, wq_a_sc
                 eta_turn(bt if u != NU + 3 else B - 1)
         b = B - 1
         clamp(b - 1, 7)
-        last_early(slice(3, 4))
-        cl = ps_c.tile([P, 2, 2, P], F32, name="ct")
+        ml = []
+        cl = []
         for k in range(2):
+            row_max(NU - 1, slice(k, k + 1))
+            qc = ps_q.tile([P, 4, P], F32)
             for hh in range(2):
-                nc.tensor.transpose(cl[:, k, hh, :], mxs[b][:, hh, 6 + k : 7 + k].to_broadcast([P, P]), ident[:])
-        ml = const.tile([P, 4, 2], F32)
-        nc.vector.tensor_reduce(out=ml[:, 0, :], in_=cl[:].rearrange("p k h r -> p k (h r)"), axis=AX.X, op=ALU.max)
-        nc.vector.scalar_tensor_tensor(out=ml[:, 1, :], in0=ml[:, 0, :], scalar=0.0, in1=ml[:, 0, :], op0=ALU.is_equal, op1=ALU.add)
-        nc.vector.reciprocal(out=ml[:, 2, :], in_=ml[:, 1, :])
-        nc.vector.tensor_scalar(out=ml[:, 3, :], in0=ml[:, 2, :], scalar1=10.0, scalar2=1.0, op0=ALU.mult, op1=ALU.min)
-        for k in range(2):
-            for gp in range(2):
-                v = st["ar", b][:, k, 2 * gp : 2 * gp + 2, :].rearrange("p g (i h d) -> p (g i) h d", i=4, h=H)[:, :, 3, :]
-                nc.vector.tensor_scalar(out=v, in0=v, scalar1=ml[:, 3, k : k + 1], scalar2=None, op0=ALU.mult)
-                for g in range(2 * gp, 2 * gp + 2):
-                    store(b, g, k, nc.sync if k == 0 else nc.scalar)
+                nc.tensor.transpose(qc[:, hh, :], mxs[b][:, hh, 6 + k : 7 + k].to_broadcast([P, P]), ident[:])
+            cl.append(qc)
+            m2 = const.tile([P, 4], F32, name="ml%d" % k)
+            ml.append(m2)
+
+        def last_max(k):
+            nc.vector.tensor_reduce(out=ml[k][:, 0:1], in_=cl[k][:, 0:2, :].rearrange("p h r -> p (h r)"), axis=AX.X, op=ALU.max)
+
+        def last_nonzero(k):
+            nc.vector.scalar_tensor_tensor(out=ml[k][:, 1:2], in0=ml[k][:, 0:1], scalar=0.0, in1=ml[k][:, 0:1], op0=ALU.is_equal, op1=ALU.add)
+
+        def last_recip(k):
+            nc.vector.reciprocal(out=ml[k][:, 2:3], in_=ml[k][:, 1:2])
+
+        def last_min(k):
+            nc.vector.tensor_scalar(out=ml[k][:, 3:4], in0=ml[k][:, 2:3], scalar1=10.0, scalar2=1.0, op0=ALU.mult, op1=ALU.min)
+
+        def last_clamp(k, gp):
+            v = st["ar", b][:, k, 2 * gp : 2 * gp + 2, :].rearrange("p g (i h d) -> p (g i) h d", i=4, h=H)[:, :, 3, :]
+            nc.vector.tensor_scalar(out=v, in0=v, scalar1=ml[k][:, 3:4], scalar2=None, op0=ALU.mult)
+            for g in range(2 * gp, 2 * gp + 2):
+                store(b, g, k, nc.sync if k == 0 else nc.scalar)
+
+        last_max(0)
+        last_early(0, slice(3, 4), "v")
+        last_nonzero(0)
+        last_max(1)
+        last_recip(0)
+        last_nonzero(1)
+        last_min(0)
+        last_recip(1)
+        last_clamp(0, 0)
+        last_min(1)
+        last_clamp(0, 1)
+        last_early(1, slice(3, 4), "v")
+        last_clamp(1, 0)
+        last_clamp(1, 1)

from contextlib import ExitStack

import concourse.mybir as mybir
from concourse.masks import make_identity

F32 = mybir.dt.float32
BF16 = mybir.dt.bfloat16
U32 = mybir.dt.uint32
I32 = mybir.dt.int32
U8 = mybir.dt.uint8
FP8 = mybir.dt.float8_e4m3fn
FP8X4 = mybir.dt.float8_e4m3fn_x4
FP4X4 = mybir.dt.float4_e2m1fn_x4
ALU = mybir.AluOpType
ACT = mybir.ActivationFunctionType
AX = mybir.AxisListType

B, S, D, H, J, QL = 4, 2048, 512, 4, 16, 512
P = 128
FLOPS = 2 * B * S * (D * QL + QL * H * 64)

GROUPS = 4
NU = B * GROUPS * 2


def tile_ssa_pa_t_w4_kernel(tc, x_bytes, x_scale, freqs_cis, wq_a_words, wq_a_scales, wq_b_words, wq_b_scales, out_0, out_1):
    nc = tc.nc
    outs = (out_0, out_1)
    with ExitStack() as ctx:
        const = ctx.enter_context(tc.tile_pool(name="const", bufs=1))
        xpool = ctx.enter_context(tc.tile_pool(name="xpool", bufs=B * GROUPS))
        work = ctx.enter_context(tc.tile_pool(name="work", bufs=3))
        res = ctx.enter_context(tc.tile_pool(name="res", bufs=3))
        ps_t = ctx.enter_context(tc.psum_pool(name="ps_t", bufs=2))
        ps_q = ctx.enter_context(tc.psum_pool(name="ps_q", bufs=3))
        ps_n = ctx.enter_context(tc.psum_pool(name="ps_n", bufs=2))
        ps_c = ctx.enter_context(tc.psum_pool(name="ps_c", bufs=1))
        ctx.enter_context(tc.manual_schedule())

        ident = const.tile([P, P], F32)
        sc = const.tile([P, 4], F32)
        wa_raw = const.tile([P, 1024], U8, align_bytes=64)
        wsa_raw = const.tile([P, 512], U8, align_bytes=64)
        wb_raw = const.tile([P, 512], U8, align_bytes=64)
        wsb_raw = const.tile([P, 256], U8, align_bytes=64)
        wa = const.tile([P, 1024], U8, align_bytes=64)
        wsa = const.tile([P, 512], U8, align_bytes=64)
        wbn = const.tile([P, 256], U8, align_bytes=64)
        wbp = const.tile([P, 256], U8, align_bytes=64)
        wsn = const.tile([P, 128], U8, align_bytes=64)
        wsp = const.tile([P, 128], U8, align_bytes=64)
        fr = const.tile([P, GROUPS, 4 * J * 2], BF16)
        cd = const.tile([P, GROUPS, 4, 2, 2, H * J], F32)
        warm = const.tile([P, 1], F32)
        mxs = []
        for b in range(B):
            mx = const.tile([P, 2, P], F32, name="mx%d" % b)
            mxs.append(mx)

        nc.vector.memset(wsa_raw[:].bitcast(I32), 0)
        nc.vector.memset(wsb_raw[:].bitcast(I32), 0)
        nc.vector.memset(warm[:], 0.0)
        nc.scalar.activation(warm[:], warm[:], func=ACT.Silu)

        xr = []

        def load_x(g, cols):
            if g == len(xr):
                xraw = xpool.tile([P, 2048], U8)
                xr.append(xraw)
            src = x_bytes[g // GROUPS, 512 * (g % GROUPS) : 512 * (g % GROUPS) + 512, :].rearrange("(p i) k -> p (i k)", i=4)
            nc.sync.dma_start(out=xr[g][:, cols], in_=src[:, cols])

        load_x(0, slice(0, 1024))
        nc.sync.dma_start(out=sc[:], in_=x_scale.rearrange("a b (p t) -> p (a b t)", t=4))
        nc.sync.dma_start(out=wa_raw[:], in_=wq_a_words[0])
        nc.sync.dma_start(out=wb_raw[:], in_=wq_b_words[0])
        load_x(0, slice(1024, 2048))
        for q in range(4):
            nc.sync.dma_start(out=wsa_raw[32 * q : 32 * q + 4, :].bitcast(I32), in_=wq_a_scales[0, 4 * q : 4 * q + 4, :].bitcast(I32))
        nc.sync.dma_start(out=fr[:], in_=freqs_cis.rearrange("(g p i) j c -> p g (i j c)", g=GROUPS, i=4))
        for q in range(4):
            nc.sync.dma_start(out=wsb_raw[32 * q : 32 * q + 4, :].bitcast(I32), in_=wq_b_scales[0, 4 * q : 4 * q + 4, :].bitcast(I32))
        for g in range(1, B * GROUPS):
            load_x(g, slice(0, 2048))

        make_identity(nc, ident[:])
        for g in range(GROUPS):
            for e in range(2):
                for k in range(2):
                    cs = 0 if e == k else 1
                    sign = -1.0 if (e == 1 and k == 0) else 1.0
                    src = fr[:, g, :].rearrange("p (i j c) -> p i j c", j=J, c=2)[:, :, :, cs]
                    nc.gpsimd.tensor_scalar(
                        out=cd[:, g, :, e, k, :].rearrange("p i (h j) -> p i h j", h=H),
                        in0=src.unsqueeze(2).to_broadcast([P, 4, H, J]),
                        scalar1=sign, scalar2=0.0, op0=ALU.mult, op1=ALU.add,
                    )
        for b in range(B):
            nc.gpsimd.memset(mxs[b][:], 0.0)

        nc.vector.tensor_copy(
            out=wa[:].rearrange("p (t m b) -> p t m b", t=4, b=2),
            in_=wa_raw[:].rearrange("p (m t b) -> p t m b", t=4, b=2),
        )
        wv = wb_raw[:].rearrange("p (h k x) -> p h k x", h=H, k=2)
        nc.vector.tensor_copy(out=wbn[:].rearrange("p (h x) -> p h x", h=H), in_=wv[:, :, 0, :])
        for e in range(2):
            nc.vector.tensor_copy(
                out=wbp[:, 128 * e : 128 * e + 128].rearrange("p (h j b) -> p h j b", h=H, b=2),
                in_=wv[:, :, 1, :].rearrange("p h (j e b) -> p h j e b", e=2, b=2)[:, :, :, e, :],
            )

        def scales_of_b():
            sv = wsb_raw[:].rearrange("p (h k x) -> p h k x", h=H, k=2)
            nc.vector.tensor_copy(out=wsn[:].rearrange("p (h x) -> p h x", h=H), in_=sv[:, :, 0, :])
            for e in range(2):
                nc.vector.tensor_copy(
                    out=wsp[:, 64 * e : 64 * e + 64].rearrange("p (h j) -> p h j", h=H),
                    in_=sv[:, :, 1, :].rearrange("p h (j e) -> p h j e", e=2)[:, :, :, e],
                )

        st = {}

        def cast(u):
            xb = work.tile([P, 1024], BF16, bufs=6)
            w = 512 if u == 0 else 1024
            for c in range(0, 1024, w):
                nc.scalar.copy(out=xb[:, c : c + w], in_=xr[u // 2][:, 1024 * (u % 2) + c : 1024 * (u % 2) + c + w].bitcast(FP8))
            st["xb", u] = xb

        def trans(u):
            words = st["xb", u][:].bitcast(F32)
            tp = ps_t.tile([P, 2, 2, P], F32)
            for i in range(2):
                for w in range(2):
                    nc.tensor.transpose(tp[:, w, i, :], words[:, 256 * i + w : 256 * (i + 1) : 2], ident[:])
            st["tp", u] = tp

        def scale_x(u):
            xg = work.tile([P, 1024], BF16, align_bytes=64)
            nc.vector.tensor_tensor(
                out=xg[:].rearrange("p (c u e) -> p c u e", u=2, e=2),
                in0=st["tp", u][:].rearrange("p u i r -> p (u i r)").bitcast(BF16).rearrange("p (u c e) -> p c u e", u=2, e=2),
                in1=sc[:].rearrange("p (o u e) -> p o u e", o=1, u=2).to_broadcast([P, 256, 2, 2]),
                op=ALU.mult,
            )
            st["xg", u] = xg

        def quant_x(u):
            xq = work.tile([P, 256], U32, align_bytes=64)
            xs = work.tile([P, 256], U8, align_bytes=64)
            nc.vector.quantize_mx(out=xq[:].bitcast(FP8X4), scales=xs[:], in_=st["xg", u][:])
            st["xq", u] = (xq, xs)

        def mm1(u):
            xq, xs = st["xq", u]
            for i in range(2):
                qc = ps_q.tile([P, 4, P], F32)
                c = slice(128 * i, 128 * i + 128)
                for t in range(4):
                    nc.tensor.matmul_mx(
                        out=qc[:, t, :],
                        lhsT=wa[:, 256 * t : 256 * t + 256].bitcast(FP4X4), lhsT_scale=wsa[:, 128 * t : 128 * t + 128],
                        rhs=xq[:, c].bitcast(FP8X4), rhs_scale=xs[:, c], start=True, stop=True,
                    )
                st["qc", u, i] = qc

        def keep_busy(u):
            ct = ps_c.tile([P, 512], F32)
            nc.tensor.matmul(ct[:], lhsT=st["xb", u][:, 0:128], rhs=st["xb", u][:, 0:512], start=True, stop=True)

        def exit_q(u):
            qg = work.tile([P, 1024], BF16, align_bytes=64)
            for i in range(2):
                nc.scalar.copy(
                    out=qg[:, 512 * i : 512 * i + 512].rearrange("p (r t) -> p r t", t=4),
                    in_=st["qc", u, i][:].rearrange("p t r -> p r t"),
                )
            st["qg", u] = qg

        def quant_q(u):
            qq = work.tile([P, 256], U32, align_bytes=64)
            qs = work.tile([P, 256], U8, align_bytes=64)
            nc.vector.quantize_mx(out=qq[:].bitcast(FP8X4), scales=qs[:], in_=st["qg", u][:])
            st["qq", u] = (qq, qs)

        def mm2(u):
            qq, qs = st["qq", u]
            nv = ps_n.tile([P, 4, P], F32)
            for k, (w, s) in enumerate(((wbn, wsn), (wbp, wsp))):
                for i in range(2):
                    c = slice(128 * i, 128 * i + 128)
                    nc.tensor.matmul_mx(
                        out=nv[:, 2 * k + i, :],
                        lhsT=qq[:, c].bitcast(FP8X4), lhsT_scale=qs[:, c],
                        rhs=w[:].bitcast(FP4X4), rhs_scale=s[:], start=True, stop=True,
                    )
            st["np", u] = nv

        def rope_mul(u, blocks):
            g, hh = (u // 2) % GROUPS, u % 2
            if blocks.start == 0:
                pt = work.tile([P, 4, 2, 64], F32)
                st["pt", u] = pt
            n = blocks.stop - blocks.start
            nc.vector.tensor_tensor(
                out=st["pt", u][:, blocks],
                in0=st["np", u][:, 2:4, :].rearrange("p i (e x) -> p (i e) x", e=2)[:, blocks].unsqueeze(2).to_broadcast([P, n, 2, 64]),
                in1=cd[:, g, 2 * hh : 2 * hh + 2, :, :, :].rearrange("p i e k x -> p (i e) k x")[:, blocks],
                op=ALU.mult,
            )

        def rope_add(u):
            pr = work.tile([P, 2, P], F32)
            v = st["pt", u][:].rearrange("p (i e) k x -> p i e (k x)", e=2)
            nc.gpsimd.tensor_tensor(out=pr[:], in0=v[:, :, 0, :], in1=v[:, :, 1, :], op=ALU.add)
            st["pr", u] = pr

        def silu_n(u):
            b, g, hh = u // 8, (u // 2) % GROUPS, u % 2
            if u % 8 == 0:
                ar = res.tile([P, 2, GROUPS, 512], F32)
                st["ar", b] = ar
            nc.scalar.activation(
                st["ar", b][:, 0, g, 256 * hh : 256 * hh + 256],
                st["np", u][:, 0:2, :].rearrange("p i x -> p (i x)"), func=ACT.Silu,
            )

        def silu_r(u):
            b, g, hh = u // 8, (u // 2) % GROUPS, u % 2
            nc.scalar.activation(
                st["ar", b][:, 1, g, 256 * hh : 256 * hh + 256].rearrange("p (i x e) -> p i x e", i=2, e=2),
                st["pr", u][:].rearrange("p i (e x) -> p i x e", e=2), func=ACT.Silu,
            )

        def row_max(u, kinds):
            b, g, hh = u // 8, (u // 2) % GROUPS, u % 2
            nc.vector.tensor_reduce(
                out=mxs[b][:, hh, 2 * g + kinds.start : 2 * g + kinds.stop],
                in_=st["ar", b][:, kinds, g, 256 * hh : 256 * hh + 256], axis=AX.X, op=ALU.max,
            )

        def eta_turn(b):
            ct = ps_c.tile([P, 512], F32)
            for hh in range(2):
                nc.tensor.transpose(ct[:, 128 * hh : 128 * hh + 128], mxs[b][:, hh, :], ident[:])
            st["ct", b] = ct

        def eta_max(b):
            m = const.tile([P, 4], F32, name="m%d" % b)
            st["m", b] = m
            nc.vector.tensor_reduce(out=m[:, 0:1], in_=st["ct", b][:, 0:256], axis=AX.X, op=ALU.max)

        def eta_nonzero(b):
            m = st["m", b]
            nc.vector.scalar_tensor_tensor(out=m[:, 1:2], in0=m[:, 0:1], scalar=0.0, in1=m[:, 0:1], op0=ALU.is_equal, op1=ALU.add)

        def eta_recip(b):
            m = st["m", b]
            nc.vector.reciprocal(out=m[:, 2:3], in_=m[:, 1:2])

        def eta_min(b):
            m = st["m", b]
            nc.vector.tensor_scalar(out=m[:, 3:4], in0=m[:, 2:3], scalar1=10.0, scalar2=1.0, op0=ALU.mult, op1=ALU.min)

        def eta_spread(b):
            ce = ps_c.tile([P, 512], F32, name="ct")
            nc.tensor.transpose(ce[:, 0:128], st["m", b][:, 3:4].to_broadcast([P, P]), ident[:])
            st["ce", b] = ce

        def eta_out(b):
            eb = const.tile([P, 8], F32, name="eb%d" % b)
            nc.scalar.copy(out=eb[:], in_=st["ce", b][:, 0:8])
            st["eb", b] = eb

        def clamp(b, step):
            h, k = step % 4, step // 4
            v = st["ar", b][:, k, :, :].rearrange("p g (i h d) -> p (g i) h d", i=4, h=H)[:, :, h, :]
            e = st["eb", b][:, 2 * h + k : 2 * h + k + 1]
            nc.gpsimd.tensor_scalar(out=v, in0=v, scalar1=e, scalar2=0.0, op0=ALU.mult, op1=ALU.add)
            if h == H - 1:
                for g in range(GROUPS):
                    store(b, g, k, nc.sync)

        def store(b, g, k, eng):
            eng.dma_start(
                out=outs[k][b, 512 * g : 512 * g + 512, :, :].rearrange("(p i) h d -> p (i h d)", i=4),
                in_=st["ar", b][:, k, g, :],
            )

        def last_early(k, groups, eng):
            b = B - 1
            v = st["ar", b][:, k, groups, :].rearrange("p g (i h d) -> p (g i) h d", i=4, h=H)
            for h in range(3):
                w, e = v[:, :, h, :], st["eb", b][:, 2 * h + k : 2 * h + k + 1]
                if eng == "s":
                    nc.scalar.activation(w, w, func=ACT.Copy, scale=e)
                elif eng == "g":
                    nc.gpsimd.tensor_scalar(out=w, in0=w, scalar1=e, scalar2=0.0, op0=ALU.mult, op1=ALU.add)
                else:
                    nc.vector.tensor_scalar(out=w, in0=w, scalar1=e, scalar2=None, op0=ALU.mult)

        def on(u):
            return 0 <= u < NU

        for u in range(-3, NU + 6):
            b0, r0 = divmod(u - 14, 8)
            eta_b = b0 if (r0 == 0 and 0 <= b0 < B - 1) else None
            if u == NU + 4:
                eta_b = B - 1
            b1, r1 = divmod(u - 15, 8)
            if (r1 == 0 and 0 <= b1 < B - 1) or u == NU + 5:
                eta_out(b1 if u < NU + 5 else B - 1)
            if on(u + 1):
                trans(u + 1)
            if on(u - 4):
                rope_mul(u - 4, slice(0, 3))
            if on(u - 3):
                quant_q(u - 3)
                mm2(u - 3)
            if eta_b is not None:
                eta_max(eta_b)
            if on(u - 1):
                quant_x(u - 1)
                mm1(u - 1)
                keep_busy(u - 1)
            if on(u - 2):
                exit_q(u - 2)
            if on(u - 4):
                rope_mul(u - 4, slice(3, 4))
                silu_n(u - 4)
                rope_add(u - 4)
            if on(u - 5):
                silu_r(u - 5)
            if eta_b is not None:
                eta_nonzero(eta_b)
            if u == NU + 5:
                last_early(0, slice(0, 3), "s")
                last_early(1, slice(0, 3), "g")
            if on(u - 6) and u - 6 < NU - 1:
                row_max(u - 6, slice(0, 2))
            if on(u + 3):
                cast(u + 3)
            if eta_b is not None:
                eta_recip(eta_b)
            if on(u):
                scale_x(u)
            if u == 0:
                nc.vector.tensor_copy(
                    out=wsa[:].rearrange("p (t m) -> p t m", t=4),
                    in_=wsa_raw[:].rearrange("p (m t) -> p t m", t=4),
                )
            if u == 1:
                scales_of_b()
            if eta_b is not None:
                eta_min(eta_b)
                eta_spread(eta_b)
            if 0 <= b1 < B - 1:
                clamp(b1, r1)
            bt, rt = divmod(u - 13, 8)
            if (rt == 0 and 0 <= bt < B - 1) or u == NU + 3:
                eta_turn(bt if u != NU + 3 else B - 1)
        b = B - 1
        clamp(b - 1, 7)
        ml = []
        cl = []
        for k in range(2):
            row_max(NU - 1, slice(k, k + 1))
            qc = ps_q.tile([P, 4, P], F32)
            for hh in range(2):
                nc.tensor.transpose(qc[:, hh, :], mxs[b][:, hh, 6 + k : 7 + k].to_broadcast([P, P]), ident[:])
            cl.append(qc)
            m2 = const.tile([P, 4], F32, name="ml%d" % k)
            ml.append(m2)

        def last_max(k):
            nc.vector.tensor_reduce(out=ml[k][:, 0:1], in_=cl[k][:, 0:2, :].rearrange("p h r -> p (h r)"), axis=AX.X, op=ALU.max)

        def last_nonzero(k):
            nc.vector.scalar_tensor_tensor(out=ml[k][:, 1:2], in0=ml[k][:, 0:1], scalar=0.0, in1=ml[k][:, 0:1], op0=ALU.is_equal, op1=ALU.add)

        def last_recip(k):
            nc.vector.reciprocal(out=ml[k][:, 2:3], in_=ml[k][:, 1:2])

        def last_min(k):
            nc.vector.tensor_scalar(out=ml[k][:, 3:4], in0=ml[k][:, 2:3], scalar1=10.0, scalar2=1.0, op0=ALU.mult, op1=ALU.min)

        def last_clamp(k, gp):
            v = st["ar", b][:, k, 2 * gp : 2 * gp + 2, :].rearrange("p g (i h d) -> p (g i) h d", i=4, h=H)[:, :, 3, :]
            nc.vector.tensor_scalar(out=v, in0=v, scalar1=ml[k][:, 3:4], scalar2=None, op0=ALU.mult)
            for g in range(2 * gp, 2 * gp + 2):
                store(b, g, k, nc.sync if k == 0 else nc.scalar)

        last_max(0)
        last_early(0, slice(3, 4), "v")
        last_nonzero(0)
        last_max(1)
        last_recip(0)
        last_nonzero(1)
        last_min(0)
        last_recip(1)
        last_clamp(0, 0)
        last_min(1)
        last_clamp(0, 1)
        last_early(1, slice(3, 4), "v")
        last_clamp(1, 0)
        last_clamp(1, 1)
